import numpy as np
import ml_dtypes


def mxq(x, axis, fmt="e4m3"):
    dtype, down = {"e4m3": (ml_dtypes.float8_e4m3fn, 7), "e5m2": (ml_dtypes.float8_e5m2, 14)}[fmt]
    v = np.moveaxis(np.asarray(x, np.float32).astype(ml_dtypes.bfloat16).astype(np.float64), axis, -1)
    blocks = v.reshape(v.shape[:-1] + (-1, 32))
    amax = np.abs(blocks).max(-1, keepdims=True)
    byte = np.maximum(np.where(amax > 0, np.frexp(amax)[1] - 1 + 127, 0) - down, 1)
    scale = np.exp2(byte - 127.0)
    codes = (blocks / scale).astype(np.float32).astype(dtype).astype(np.float64)
    return np.moveaxis((codes * scale).reshape(v.shape), -1, axis)


WIDE = False


def mx_kscale(k):
    if not WIDE:
        return np.ones(k)
    levels = np.array([10, -10, 5, -5, 0])
    a = np.random.permutation(np.resize(levels, k // 512 * 4)).reshape(k // 512, 4)
    idx = np.arange(k)
    return np.exp2(a[idx // 512, idx % 128 // 32])


BF16 = ml_dtypes.bfloat16


def bf(x):
    return np.asarray(x, np.float32).astype(BF16)


def f64(x):
    return np.asarray(x).astype(np.float64)


B, D_IN, D_H, W_RANK, U_RANK = 4096, 1024, 1024, 512, 512


def sigmoid(v):
    return 1.0 / (1.0 + np.exp(-v))


def setup_inputs():
    s, t = mx_kscale(W_RANK), mx_kscale(U_RANK)
    return {
        "wx_r": bf(np.random.standard_normal((B, W_RANK)) * s),
        "uh_r": bf(np.random.standard_normal((B, U_RANK)) * t),
        "state": bf(np.random.standard_normal((B, D_H))),
        "W2": bf(np.random.standard_normal((D_H, W_RANK)) * 0.7 / np.sqrt(W_RANK) / s),
        "U2": bf(np.random.standard_normal((D_H, U_RANK)) * 0.7 / np.sqrt(U_RANK) / t),
        "bias_gate": bf(1.0 + 0.5 * np.random.standard_normal((1, D_H))),
        "bias_update": bf(1.0 + 0.5 * np.random.standard_normal((1, D_H))),
        "zeta": bf(1.0 + 0.1 * np.random.standard_normal((1, 1))),
        "nu": bf(-1.5 + 0.1 * np.random.standard_normal((1, 1))),
    }


def reference(wx_r, uh_r, state, W2, U2, bias_gate, bias_update, zeta, nu):
    wx = mxq(f64(wx_r), 1, "e4m3") @ mxq(f64(W2), 1, "e4m3").T
    uh = mxq(f64(uh_r), 1, "e4m3") @ mxq(f64(U2), 1, "e4m3").T
    pre = wx + uh
    z = sigmoid(pre + f64(bias_gate))
    h_cand = np.tanh(pre + f64(bias_update))
    return z * f64(state) + (sigmoid(f64(zeta)) * (1.0 - z) + sigmoid(f64(nu))) * h_cand

@@ -1,0 +1,270 @@
+from contextlib import ExitStack
+
+import concourse.mybir as mybir
+from concourse.masks import make_identity
+
+F32 = mybir.dt.float32
+BF16 = mybir.dt.bfloat16
+U32 = mybir.dt.uint32
+U8 = mybir.dt.uint8
+FP8X4 = mybir.dt.float8_e4m3fn_x4
+ACT = mybir.ActivationFunctionType
+ALU = mybir.AluOpType
+
+P = 128
+PACK = 4
+BATCH, RANK, HIDDEN = 4096, 512, 1024
+ROWS = 512
+BLOCKS = ROWS // P
+CHUNKS = BATCH // ROWS
+HALVES = HIDDEN // ROWS
+UNITS = CHUNKS * HALVES
+WORDS = RANK // 2
+RAW_BUFS = 6
+FIRST_STEPS = 8
+LEAD = 14
+TINY = 1e-30
+
+FLOPS = 2 * BATCH * HIDDEN * (2 * RANK)
+
+
+def tile_fastgrnncudacell_pa_t_kernel(
+    tc, wx_r, uh_r, state, W2, U2, bias_gate, bias_update, zeta, nu, out
+):
+    nc = tc.nc
+    with ExitStack() as ctx:
+        const = ctx.enter_context(tc.tile_pool(name="const", bufs=1))
+        raw_pool = ctx.enter_context(tc.tile_pool(name="raw", bufs=RAW_BUFS))
+        grouped_pool = ctx.enter_context(tc.tile_pool(name="grouped", bufs=3))
+        moving_pool = ctx.enter_context(tc.tile_pool(name="moving", bufs=2))
+        state_pool = ctx.enter_context(tc.tile_pool(name="state", bufs=3))
+        gates_pool = ctx.enter_context(tc.tile_pool(name="gates", bufs=4))
+        out_pool = ctx.enter_context(tc.tile_pool(name="outp", bufs=2))
+        psum_pre = ctx.enter_context(tc.psum_pool(name="psum_pre", bufs=2))
+        psum_fwd = ctx.enter_context(tc.psum_pool(name="psum_fwd", bufs=1))
+        psum_back = ctx.enter_context(tc.psum_pool(name="psum_back", bufs=5))
+        ctx.enter_context(tc.manual_schedule())
+
+        batch_view = "(c p i) d -> c p (i d)"
+        state_v = state.rearrange(batch_view, p=P, i=BLOCKS)
+        out_v = out.rearrange(batch_view, p=P, i=BLOCKS)
+        weight_view = "(h q p) k -> h p q k"
+        sources = {
+            "wx": wx_r.rearrange(batch_view, p=P, i=BLOCKS),
+            "uh": uh_r.rearrange(batch_view, p=P, i=BLOCKS),
+            "w2": W2.rearrange(weight_view, q=BLOCKS, p=P),
+            "u2": U2.rearrange(weight_view, q=BLOCKS, p=P),
+        }
+        operands = [("w2", 0), ("wx", 0), ("u2", 0), ("uh", 0), ("w2", 1), ("u2", 1)]
+        for c in range(1, CHUNKS):
+            operands.extend([("wx", c), ("uh", c)])
+        total_steps = 2 * len(operands)
+
+        raw = {}
+        grouped = {}
+        codes = {}
+        scales = {}
+
+        def load_operand(k):
+            kind, index = operands[k]
+            raw[k] = raw_pool.tile([P, BLOCKS * RANK], BF16, name="raw", tag="raw")
+            if kind in ("wx", "uh"):
+                nc.sync.dma_start(out=raw[k][:], in_=sources[kind][index])
+            else:
+                nc.sync.dma_start(
+                    out=raw[k][:].rearrange("p (q k) -> p q k", q=BLOCKS),
+                    in_=sources[kind][index],
+                )
+
+        def load_state(c):
+            state_sb[c] = state_pool.tile([P, BLOCKS * HIDDEN], BF16, name="state_sb", tag="state_sb")
+            nc.sync.dma_start(out=state_sb[c][:], in_=state_v[c])
+
+        def transpose_step(s, on_vector):
+            k, a = divmod(s, 2)
+            if a == 0:
+                grouped[k] = grouped_pool.tile(
+                    [P, ROWS * PACK], BF16, name="grouped", tag="grouped", align_bytes=64
+                )
+            words = raw[k][:].bitcast(F32)
+            flipped = psum_fwd.tile([P, 2 * 2 * P], F32, name="flipped", tag="flipped")
+            for v in range(2):
+                for j in range(2):
+                    block = 2 * a + j
+                    nc.tensor.transpose(
+                        flipped[:, (2 * v + j) * P : (2 * v + j + 1) * P],
+                        words[:, block * WORDS + v * P : block * WORDS + (v + 1) * P],
+                        ident[:],
+                    )
+            dst = grouped[k][:].bitcast(F32).rearrange("p (n v) -> p n v", v=2)
+            dst = dst[:, 2 * a * P : 2 * (a + 1) * P, :]
+            src = flipped[:].rearrange("p (v n) -> p n v", v=2)
+            if on_vector:
+                nc.vector.tensor_copy(out=dst, in_=src)
+            else:
+                nc.scalar.copy(out=dst, in_=src)
+            if a == 1 and k + RAW_BUFS < len(operands):
+                load_operand(k + RAW_BUFS)
+
+        def quantise(k):
+            kind, index = operands[k]
+            if kind in ("wx", "uh"):
+                pool, tag = moving_pool, kind
+            else:
+                pool, tag = const, "%s%d" % (kind, index)
+            codes[operands[k]] = pool.tile(
+                [P, ROWS], U32, name="codes_" + tag, tag="codes_" + tag, align_bytes=64
+            )
+            scales[operands[k]] = pool.tile(
+                [P, ROWS], U8, name="scales_" + tag, tag="scales_" + tag, align_bytes=64
+            )
+            nc.vector.quantize_mx(
+                out=codes[operands[k]][:].bitcast(FP8X4),
+                scales=scales[operands[k]][:],
+                in_=grouped[k][:],
+            )
+
+        gate_t = {}
+        cand_t = {}
+        state_sb = {}
+        out_sb = {}
+
+        def project(u, a):
+            c, h = divmod(u, HALVES)
+            if a == 0:
+                gate_t[u] = gates_pool.tile([P, BLOCKS * ROWS], F32, name="gate_t", tag="gate_t")
+                cand_t[u] = gates_pool.tile([P, BLOCKS * ROWS], F32, name="cand_t", tag="cand_t")
+            for q in (2 * a, 2 * a + 1):
+                m = BLOCKS * h + q
+                pre = psum_pre.tile([P, ROWS], F32, name="pre", tag="pre")
+                pairs = ((("w2", h), ("wx", c)), (("u2", h), ("uh", c)))
+                for n, (weight, moving) in enumerate(pairs):
+                    nc.tensor.matmul_mx(
+                        out=pre[:],
+                        lhsT=codes[weight][:, q * P : (q + 1) * P].bitcast(FP8X4),
+                        lhsT_scale=scales[weight][:, q * P : (q + 1) * P],
+                        rhs=codes[moving][:].bitcast(FP8X4),
+                        rhs_scale=scales[moving][:],
+                        start=(n == 0),
+                        stop=(n == 1),
+                    )
+                cols = slice(q * ROWS, (q + 1) * ROWS)
+                nc.scalar.activation(
+                    out=gate_t[u][:, cols], in_=pre[:], func=ACT.Sigmoid,
+                    bias=bias_t[:, m : m + 1], scale=1.0,
+                )
+                nc.scalar.activation(
+                    out=cand_t[u][:, cols], in_=pre[:], func=ACT.Tanh,
+                    bias=bias_t[:, 2 * BLOCKS + m : 2 * BLOCKS + m + 1], scale=1.0,
+                )
+
+        def candidate_term(u, a):
+            cols = slice(2 * a * ROWS, 2 * (a + 1) * ROWS)
+            nc.vector.scalar_tensor_tensor(
+                out=cand_t[u][:, cols], in0=gate_t[u][:, cols], scalar=kappa[:, 0:1],
+                in1=cand_t[u][:, cols], op0=ALU.subtract, op1=ALU.mult,
+            )
+
+        def transpose_back(u, a):
+            banks = []
+            for source in (gate_t[u], cand_t[u]):
+                for j in range(2):
+                    i = 2 * a + j
+                    bank = psum_back.tile([P, ROWS], F32, name="bank", tag="bank")
+                    for q in range(BLOCKS):
+                        nc.tensor.transpose(
+                            bank[:, q * P : (q + 1) * P],
+                            source[:, q * ROWS + i * P : q * ROWS + (i + 1) * P],
+                            ident[:],
+                        )
+                    banks.append(bank)
+            return banks
+
+        def mix(u, a, banks):
+            c, h = divmod(u, HALVES)
+            if h == 0 and a == 0:
+                out_sb[c] = out_pool.tile([P, BLOCKS * HIDDEN], F32, name="out_sb", tag="out_sb")
+            spans = [
+                slice((2 * a + j) * HIDDEN + h * ROWS, (2 * a + j) * HIDDEN + (h + 1) * ROWS)
+                for j in range(2)
+            ]
+            for j in range(2):
+                nc.vector.tensor_tensor(
+                    out=out_sb[c][:, spans[j]], in0=banks[j][:], in1=state_sb[c][:, spans[j]],
+                    op=ALU.mult,
+                )
+            for j in range(2):
+                nc.vector.scalar_tensor_tensor(
+                    out=out_sb[c][:, spans[j]], in0=banks[2 + j][:], scalar=neg_sz[:, 0:1],
+                    in1=out_sb[c][:, spans[j]], op0=ALU.mult, op1=ALU.add,
+                )
+            if h == HALVES - 1:
+                done = slice(2 * a * HIDDEN, 2 * (a + 1) * HIDDEN)
+                nc.sync.dma_start(out=out_v[c][:, done], in_=out_sb[c][:, done])
+
+        for k in range(4):
+            load_operand(k)
+        zeta_sb = const.tile([P, 1], BF16, name="zeta_sb")
+        nu_sb = const.tile([P, 1], BF16, name="nu_sb")
+        bias_rows = const.tile([P, P], BF16, name="bias_rows")
+        nc.gpsimd.memset(bias_rows[:], 0.0)
+        nc.scalar.dma_start(out=zeta_sb[:], in_=zeta.to_broadcast([P, 1]))
+        nc.scalar.dma_start(out=nu_sb[:], in_=nu.to_broadcast([P, 1]))
+        row_view = "o (m p) -> (o m) p"
+        nc.scalar.dma_start(out=bias_rows[0 : 2 * BLOCKS, :], in_=bias_gate.rearrange(row_view, p=P))
+        nc.scalar.dma_start(
+            out=bias_rows[2 * BLOCKS : 4 * BLOCKS, :], in_=bias_update.rearrange(row_view, p=P)
+        )
+        for k in range(4, RAW_BUFS):
+            load_operand(k)
+        load_state(0)
+
+        ident = const.tile([P, P], F32, name="ident")
+        make_identity(nc, ident[:])
+
+        sz = const.tile([P, 1], F32, name="sz")
+        sn = const.tile([P, 1], F32, name="sn")
+        inv_sz = const.tile([P, 1], F32, name="inv_sz")
+        kappa = const.tile([P, 1], F32, name="kappa")
+        neg_sz = const.tile([P, 1], F32, name="neg_sz")
+        nc.scalar.activation(out=sz[:], in_=zeta_sb[:], func=ACT.Sigmoid)
+        nc.scalar.activation(out=sn[:], in_=nu_sb[:], func=ACT.Sigmoid)
+        nc.vector.tensor_scalar_max(out=sz[:], in0=sz[:], scalar1=TINY)
+        nc.vector.reciprocal(out=inv_sz[:], in_=sz[:])
+        nc.vector.tensor_add(out=kappa[:], in0=sz[:], in1=sn[:])
+        nc.vector.tensor_mul(out=kappa[:], in0=kappa[:], in1=inv_sz[:])
+        nc.vector.tensor_scalar_mul(out=neg_sz[:], in0=sz[:], scalar1=-1.0)
+
+        bias_rows_f = const.tile([P, P], F32, name="bias_rows_f")
+        bias_t = const.tile([P, 4 * BLOCKS], F32, name="bias_t")
+        nc.vector.tensor_copy(out=bias_rows_f[:], in_=bias_rows[:])
+        bias_ps = psum_fwd.tile([P, 2 * 2 * P], F32, name="bias_ps", tag="flipped")
+        nc.tensor.transpose(bias_ps[:, 0:P], bias_rows_f[:], ident[:])
+        nc.vector.tensor_copy(out=bias_t[:], in_=bias_ps[:, 0 : 4 * BLOCKS])
+
+        for s in range(FIRST_STEPS):
+            transpose_step(s, on_vector=(s % 2 == 1))
+            if s % 2 == 1:
+                quantise(s // 2)
+        steps_done = FIRST_STEPS
+
+        for t in range(2 * (UNITS + 2)):
+            u, a = divmod(t, 2)
+            if t % (2 * HALVES) == 0 and t // (2 * HALVES) + 1 < CHUNKS:
+                load_state(t // (2 * HALVES) + 1)
+            if u < UNITS:
+                project(u, a)
+            banks = transpose_back(u - 2, a) if u >= 2 else None
+            steps_due = min(total_steps, steps_done + 2, t + 1 + LEAD)
+            finished = []
+            while steps_done < steps_due:
+                transpose_step(steps_done, on_vector=(u < 2))
+                if steps_done % 2 == 1:
+                    finished.append(steps_done // 2)
+                steps_done += 1
+            if u >= 2:
+                mix(u - 2, a, banks)
+            if 1 <= u <= UNITS:
+                candidate_term(u - 1, a)
+            for k in finished:
+                quantise(k)

@@ -129,34 +129,33 @@ def tile_fastgrnncudacell_pa_t_kernel(
         state_sb = {}
         out_sb = {}
 
-        def project(u, a):
+        def project(u, q):
             c, h = divmod(u, HALVES)
-            if a == 0:
+            if q == 0:
                 gate_t[u] = gates_pool.tile([P, BLOCKS * ROWS], F32, name="gate_t", tag="gate_t")
                 cand_t[u] = gates_pool.tile([P, BLOCKS * ROWS], F32, name="cand_t", tag="cand_t")
-            for q in (2 * a, 2 * a + 1):
-                m = BLOCKS * h + q
-                pre = psum_pre.tile([P, ROWS], F32, name="pre", tag="pre")
-                pairs = ((("w2", h), ("wx", c)), (("u2", h), ("uh", c)))
-                for n, (weight, moving) in enumerate(pairs):
-                    nc.tensor.matmul_mx(
-                        out=pre[:],
-                        lhsT=codes[weight][:, q * P : (q + 1) * P].bitcast(FP8X4),
-                        lhsT_scale=scales[weight][:, q * P : (q + 1) * P],
-                        rhs=codes[moving][:].bitcast(FP8X4),
-                        rhs_scale=scales[moving][:],
-                        start=(n == 0),
-                        stop=(n == 1),
-                    )
-                cols = slice(q * ROWS, (q + 1) * ROWS)
-                nc.scalar.activation(
-                    out=gate_t[u][:, cols], in_=pre[:], func=ACT.Sigmoid,
-                    bias=bias_t[:, m : m + 1], scale=1.0,
+            m = BLOCKS * h + q
+            pre = psum_pre.tile([P, ROWS], F32, name="pre", tag="pre")
+            pairs = ((("w2", h), ("wx", c)), (("u2", h), ("uh", c)))
+            for n, (weight, moving) in enumerate(pairs):
+                nc.tensor.matmul_mx(
+                    out=pre[:],
+                    lhsT=codes[weight][:, q * P : (q + 1) * P].bitcast(FP8X4),
+                    lhsT_scale=scales[weight][:, q * P : (q + 1) * P],
+                    rhs=codes[moving][:].bitcast(FP8X4),
+                    rhs_scale=scales[moving][:],
+                    start=(n == 0),
+                    stop=(n == 1),
                 )
-                nc.scalar.activation(
-                    out=cand_t[u][:, cols], in_=pre[:], func=ACT.Tanh,
-                    bias=bias_t[:, 2 * BLOCKS + m : 2 * BLOCKS + m + 1], scale=1.0,
-                )
+            cols = slice(q * ROWS, (q + 1) * ROWS)
+            nc.scalar.activation(
+                out=gate_t[u][:, cols], in_=pre[:], func=ACT.Sigmoid,
+                bias=bias_t[:, m : m + 1], scale=1.0,
+            )
+            nc.scalar.activation(
+                out=cand_t[u][:, cols], in_=pre[:], func=ACT.Tanh,
+                bias=bias_t[:, 2 * BLOCKS + m : 2 * BLOCKS + m + 1], scale=1.0,
+            )
 
         def candidate_term(u, a):
             cols = slice(2 * a * ROWS, 2 * (a + 1) * ROWS)
@@ -165,19 +164,18 @@ def tile_fastgrnncudacell_pa_t_kernel(
                 in1=cand_t[u][:, cols], op0=ALU.subtract, op1=ALU.mult,
             )
 
-        def transpose_back(u, a):
+        def transpose_back(source, a):
             banks = []
-            for source in (gate_t[u], cand_t[u]):
-                for j in range(2):
-                    i = 2 * a + j
-                    bank = psum_back.tile([P, ROWS], F32, name="bank", tag="bank")
-                    for q in range(BLOCKS):
-                        nc.tensor.transpose(
-                            bank[:, q * P : (q + 1) * P],
-                            source[:, q * ROWS + i * P : q * ROWS + (i + 1) * P],
-                            ident[:],
-                        )
-                    banks.append(bank)
+            for j in range(2):
+                i = 2 * a + j
+                bank = psum_back.tile([P, ROWS], F32, name="bank", tag="bank")
+                for q in range(BLOCKS):
+                    nc.tensor.transpose(
+                        bank[:, q * P : (q + 1) * P],
+                        source[:, q * ROWS + i * P : q * ROWS + (i + 1) * P],
+                        ident[:],
+                    )
+                banks.append(bank)
             return banks
 
         def mix(u, a, banks):
@@ -252,9 +250,15 @@ def tile_fastgrnncudacell_pa_t_kernel(
             u, a = divmod(t, 2)
             if t % (2 * HALVES) == 0 and t // (2 * HALVES) + 1 < CHUNKS:
                 load_state(t // (2 * HALVES) + 1)
+            banks = []
             if u < UNITS:
-                project(u, a)
-            banks = transpose_back(u - 2, a) if u >= 2 else None
+                project(u, 2 * a)
+            if u >= 2:
+                banks.extend(transpose_back(gate_t[u - 2], a))
+            if u < UNITS:
+                project(u, 2 * a + 1)
+            if u >= 2:
+                banks.extend(transpose_back(cand_t[u - 2], a))
             steps_due = min(total_steps, steps_done + 2, t + 1 + LEAD)
             finished = []
             while steps_done < steps_due:

@@ -40,6 +40,7 @@ def tile_fastgrnncudacell_pa_t_kernel(
         state_pool = ctx.enter_context(tc.tile_pool(name="state", bufs=3))
         gates_pool = ctx.enter_context(tc.tile_pool(name="gates", bufs=4))
         out_pool = ctx.enter_context(tc.tile_pool(name="outp", bufs=2))
+        shift_pool = ctx.enter_context(tc.tile_pool(name="shift", bufs=2))
         psum_pre = ctx.enter_context(tc.psum_pool(name="psum_pre", bufs=2))
         psum_fwd = ctx.enter_context(tc.psum_pool(name="psum_fwd", bufs=1))
         psum_back = ctx.enter_context(tc.psum_pool(name="psum_back", bufs=5))
@@ -159,9 +160,13 @@ def tile_fastgrnncudacell_pa_t_kernel(
 
         def candidate_term(u, a):
             cols = slice(2 * a * ROWS, 2 * (a + 1) * ROWS)
-            nc.vector.scalar_tensor_tensor(
-                out=cand_t[u][:, cols], in0=gate_t[u][:, cols], scalar=kappa[:, 0:1],
-                in1=cand_t[u][:, cols], op0=ALU.subtract, op1=ALU.mult,
+            shifted = shift_pool.tile([P, 2 * ROWS], F32, name="shifted", tag="shifted")
+            nc.gpsimd.tensor_scalar(
+                out=shifted[:], in0=gate_t[u][:, cols], scalar1=one[:, 0:1],
+                scalar2=neg_kappa[:, 0:1], op0=ALU.mult, op1=ALU.add,
+            )
+            nc.gpsimd.tensor_tensor(
+                out=cand_t[u][:, cols], in0=shifted[:], in1=cand_t[u][:, cols], op=ALU.mult
             )
 
         def transpose_back(source, a):
@@ -232,6 +237,10 @@ def tile_fastgrnncudacell_pa_t_kernel(
         nc.vector.tensor_add(out=kappa[:], in0=sz[:], in1=sn[:])
         nc.vector.tensor_mul(out=kappa[:], in0=kappa[:], in1=inv_sz[:])
         nc.vector.tensor_scalar_mul(out=neg_sz[:], in0=sz[:], scalar1=-1.0)
+        neg_kappa = const.tile([P, 1], F32, name="neg_kappa")
+        one = const.tile([P, 1], F32, name="one")
+        nc.vector.tensor_scalar_mul(out=neg_kappa[:], in0=kappa[:], scalar1=-1.0)
+        nc.vector.memset(one[:], 1.0)
 
         bias_rows_f = const.tile([P, P], F32, name="bias_rows_f")
         bias_t = const.tile([P, 4 * BLOCKS], F32, name="bias_t")

@@ -159,8 +159,13 @@ def tile_fastgrnncudacell_pa_t_kernel(
             )
 
         def candidate_term(u, a):
-            cols = slice(2 * a * ROWS, 2 * (a + 1) * ROWS)
-            shifted = shift_pool.tile([P, 2 * ROWS], F32, name="shifted", tag="shifted")
+            cols = slice(2 * a * ROWS, (2 * a + 1) * ROWS)
+            nc.vector.scalar_tensor_tensor(
+                out=cand_t[u][:, cols], in0=gate_t[u][:, cols], scalar=kappa[:, 0:1],
+                in1=cand_t[u][:, cols], op0=ALU.subtract, op1=ALU.mult,
+            )
+            cols = slice((2 * a + 1) * ROWS, (2 * a + 2) * ROWS)
+            shifted = shift_pool.tile([P, ROWS], F32, name="shifted", tag="shifted")
             nc.gpsimd.tensor_scalar(
                 out=shifted[:], in0=gate_t[u][:, cols], scalar1=one[:, 0:1],
                 scalar2=neg_kappa[:, 0:1], op0=ALU.mult, op1=ALU.add,

@@ -23,6 +23,8 @@ WORDS = RANK // 2
 RAW_BUFS = 6
 FIRST_STEPS = 8
 LEAD = 14
+ROUNDS = 2 * UNITS
+LAG = 3
 TINY = 1e-30
 
 FLOPS = 2 * BATCH * HIDDEN * (2 * RANK)
@@ -260,29 +262,31 @@ def tile_fastgrnncudacell_pa_t_kernel(
                 quantise(s // 2)
         steps_done = FIRST_STEPS
 
-        for t in range(2 * (UNITS + 2)):
+        for t in range(ROUNDS + LAG):
             u, a = divmod(t, 2)
+            mixing = t >= LAG
+            mixed_u, mixed_a = divmod(t - LAG, 2)
             if t % (2 * HALVES) == 0 and t // (2 * HALVES) + 1 < CHUNKS:
                 load_state(t // (2 * HALVES) + 1)
             banks = []
-            if u < UNITS:
+            if t < ROUNDS:
                 project(u, 2 * a)
-            if u >= 2:
-                banks.extend(transpose_back(gate_t[u - 2], a))
-            if u < UNITS:
+            if mixing:
+                banks.extend(transpose_back(gate_t[mixed_u], mixed_a))
+            if t < ROUNDS:
                 project(u, 2 * a + 1)
-            if u >= 2:
-                banks.extend(transpose_back(cand_t[u - 2], a))
+            if mixing:
+                banks.extend(transpose_back(cand_t[mixed_u], mixed_a))
             steps_due = min(total_steps, steps_done + 2, t + 1 + LEAD)
             finished = []
             while steps_done < steps_due:
-                transpose_step(steps_done, on_vector=(u < 2))
+                transpose_step(steps_done, on_vector=(not mixing))
                 if steps_done % 2 == 1:
                     finished.append(steps_done // 2)
                 steps_done += 1
-            if u >= 2:
-                mix(u - 2, a, banks)
-            if 1 <= u <= UNITS:
-                candidate_term(u - 1, a)
+            if 1 <= t <= ROUNDS:
+                candidate_term((t - 1) // 2, (t - 1) % 2)
+            if mixing:
+                mix(mixed_u, mixed_a, banks)
             for k in finished:
                 quantise(k)

@@ -24,7 +24,7 @@ RAW_BUFS = 6
 FIRST_STEPS = 8
 LEAD = 14
 ROUNDS = 2 * UNITS
-LAG = 3
+LAG = 4
 TINY = 1e-30
 
 FLOPS = 2 * BATCH * HIDDEN * (2 * RANK)
@@ -190,23 +190,26 @@ def tile_fastgrnncudacell_pa_t_kernel(
                 banks.append(bank)
             return banks
 
-        def mix(u, a, banks):
+        def span(u, a, j):
+            start = (2 * a + j) * HIDDEN + (u % HALVES) * ROWS
+            return slice(start, start + ROWS)
+
+        def gate_times_state(u, a, banks):
             c, h = divmod(u, HALVES)
             if h == 0 and a == 0:
                 out_sb[c] = out_pool.tile([P, BLOCKS * HIDDEN], F32, name="out_sb", tag="out_sb")
-            spans = [
-                slice((2 * a + j) * HIDDEN + h * ROWS, (2 * a + j) * HIDDEN + (h + 1) * ROWS)
-                for j in range(2)
-            ]
             for j in range(2):
                 nc.vector.tensor_tensor(
-                    out=out_sb[c][:, spans[j]], in0=banks[j][:], in1=state_sb[c][:, spans[j]],
-                    op=ALU.mult,
+                    out=out_sb[c][:, span(u, a, j)], in0=banks[j][:],
+                    in1=state_sb[c][:, span(u, a, j)], op=ALU.mult,
                 )
+
+        def add_candidate(u, a, banks):
+            c, h = divmod(u, HALVES)
             for j in range(2):
                 nc.vector.scalar_tensor_tensor(
-                    out=out_sb[c][:, spans[j]], in0=banks[2 + j][:], scalar=neg_sz[:, 0:1],
-                    in1=out_sb[c][:, spans[j]], op0=ALU.mult, op1=ALU.add,
+                    out=out_sb[c][:, span(u, a, j)], in0=banks[j][:], scalar=neg_sz[:, 0:1],
+                    in1=out_sb[c][:, span(u, a, j)], op0=ALU.mult, op1=ALU.add,
                 )
             if h == HALVES - 1:
                 done = slice(2 * a * HIDDEN, 2 * (a + 1) * HIDDEN)
@@ -268,15 +271,14 @@ def tile_fastgrnncudacell_pa_t_kernel(
             mixed_u, mixed_a = divmod(t - LAG, 2)
             if t % (2 * HALVES) == 0 and t // (2 * HALVES) + 1 < CHUNKS:
                 load_state(t // (2 * HALVES) + 1)
-            banks = []
             if t < ROUNDS:
                 project(u, 2 * a)
             if mixing:
-                banks.extend(transpose_back(gate_t[mixed_u], mixed_a))
+                gate_banks = transpose_back(gate_t[mixed_u], mixed_a)
             if t < ROUNDS:
                 project(u, 2 * a + 1)
             if mixing:
-                banks.extend(transpose_back(cand_t[mixed_u], mixed_a))
+                cand_banks = transpose_back(cand_t[mixed_u], mixed_a)
             steps_due = min(total_steps, steps_done + 2, t + 1 + LEAD)
             finished = []
             while steps_done < steps_due:
@@ -284,9 +286,11 @@ def tile_fastgrnncudacell_pa_t_kernel(
                 if steps_done % 2 == 1:
                     finished.append(steps_done // 2)
                 steps_done += 1
+            if mixing:
+                gate_times_state(mixed_u, mixed_a, gate_banks)
             if 1 <= t <= ROUNDS:
                 candidate_term((t - 1) // 2, (t - 1) % 2)
             if mixing:
-                mix(mixed_u, mixed_a, banks)
+                add_candidate(mixed_u, mixed_a, cand_banks)
             for k in finished:
                 quantise(k)

from contextlib import ExitStack

import concourse.mybir as mybir
from concourse.masks import make_identity

F32 = mybir.dt.float32
BF16 = mybir.dt.bfloat16
U32 = mybir.dt.uint32
U8 = mybir.dt.uint8
FP8X4 = mybir.dt.float8_e4m3fn_x4
ACT = mybir.ActivationFunctionType
ALU = mybir.AluOpType

P = 128
PACK = 4
BATCH, RANK, HIDDEN = 4096, 512, 1024
ROWS = 512
BLOCKS = ROWS // P
CHUNKS = BATCH // ROWS
HALVES = HIDDEN // ROWS
UNITS = CHUNKS * HALVES
WORDS = RANK // 2
RAW_BUFS = 6
FIRST_STEPS = 8
LEAD = 14
ROUNDS = 2 * UNITS
LAG = 4
TINY = 1e-30

FLOPS = 2 * BATCH * HIDDEN * (2 * RANK)


def tile_fastgrnncudacell_pa_t_kernel(
    tc, wx_r, uh_r, state, W2, U2, bias_gate, bias_update, zeta, nu, out
):
    nc = tc.nc
    with ExitStack() as ctx:
        const = ctx.enter_context(tc.tile_pool(name="const", bufs=1))
        raw_pool = ctx.enter_context(tc.tile_pool(name="raw", bufs=RAW_BUFS))
        grouped_pool = ctx.enter_context(tc.tile_pool(name="grouped", bufs=3))
        moving_pool = ctx.enter_context(tc.tile_pool(name="moving", bufs=2))
        state_pool = ctx.enter_context(tc.tile_pool(name="state", bufs=3))
        gates_pool = ctx.enter_context(tc.tile_pool(name="gates", bufs=4))
        out_pool = ctx.enter_context(tc.tile_pool(name="outp", bufs=2))
        shift_pool = ctx.enter_context(tc.tile_pool(name="shift", bufs=2))
        psum_pre = ctx.enter_context(tc.psum_pool(name="psum_pre", bufs=2))
        psum_fwd = ctx.enter_context(tc.psum_pool(name="psum_fwd", bufs=1))
        psum_back = ctx.enter_context(tc.psum_pool(name="psum_back", bufs=5))
        ctx.enter_context(tc.manual_schedule())

        batch_view = "(c p i) d -> c p (i d)"
        state_v = state.rearrange(batch_view, p=P, i=BLOCKS)
        out_v = out.rearrange(batch_view, p=P, i=BLOCKS)
        weight_view = "(h q p) k -> h p q k"
        sources = {
            "wx": wx_r.rearrange(batch_view, p=P, i=BLOCKS),
            "uh": uh_r.rearrange(batch_view, p=P, i=BLOCKS),
            "w2": W2.rearrange(weight_view, q=BLOCKS, p=P),
            "u2": U2.rearrange(weight_view, q=BLOCKS, p=P),
        }
        operands = [("w2", 0), ("wx", 0), ("u2", 0), ("uh", 0), ("w2", 1), ("u2", 1)]
        for c in range(1, CHUNKS):
            operands.extend([("wx", c), ("uh", c)])
        total_steps = 2 * len(operands)

        raw = {}
        grouped = {}
        codes = {}
        scales = {}

        def load_operand(k):
            kind, index = operands[k]
            raw[k] = raw_pool.tile([P, BLOCKS * RANK], BF16, name="raw", tag="raw")
            if kind in ("wx", "uh"):
                nc.sync.dma_start(out=raw[k][:], in_=sources[kind][index])
            else:
                nc.sync.dma_start(
                    out=raw[k][:].rearrange("p (q k) -> p q k", q=BLOCKS),
                    in_=sources[kind][index],
                )

        def load_state(c):
            state_sb[c] = state_pool.tile([P, BLOCKS * HIDDEN], BF16, name="state_sb", tag="state_sb")
            nc.sync.dma_start(out=state_sb[c][:], in_=state_v[c])

        def transpose_step(s, on_vector):
            k, a = divmod(s, 2)
            if a == 0:
                grouped[k] = grouped_pool.tile(
                    [P, ROWS * PACK], BF16, name="grouped", tag="grouped", align_bytes=64
                )
            words = raw[k][:].bitcast(F32)
            flipped = psum_fwd.tile([P, 2 * 2 * P], F32, name="flipped", tag="flipped")
            for v in range(2):
                for j in range(2):
                    block = 2 * a + j
                    nc.tensor.transpose(
                        flipped[:, (2 * v + j) * P : (2 * v + j + 1) * P],
                        words[:, block * WORDS + v * P : block * WORDS + (v + 1) * P],
                        ident[:],
                    )
            dst = grouped[k][:].bitcast(F32).rearrange("p (n v) -> p n v", v=2)
            dst = dst[:, 2 * a * P : 2 * (a + 1) * P, :]
            src = flipped[:].rearrange("p (v n) -> p n v", v=2)
            if on_vector:
                nc.vector.tensor_copy(out=dst, in_=src)
            else:
                nc.scalar.copy(out=dst, in_=src)
            if a == 1 and k + RAW_BUFS < len(operands):
                load_operand(k + RAW_BUFS)

        def quantise(k):
            kind, index = operands[k]
            if kind in ("wx", "uh"):
                pool, tag = moving_pool, kind
            else:
                pool, tag = const, "%s%d" % (kind, index)
            codes[operands[k]] = pool.tile(
                [P, ROWS], U32, name="codes_" + tag, tag="codes_" + tag, align_bytes=64
            )
            scales[operands[k]] = pool.tile(
                [P, ROWS], U8, name="scales_" + tag, tag="scales_" + tag, align_bytes=64
            )
            nc.vector.quantize_mx(
                out=codes[operands[k]][:].bitcast(FP8X4),
                scales=scales[operands[k]][:],
                in_=grouped[k][:],
            )

        gate_t = {}
        cand_t = {}
        state_sb = {}
        out_sb = {}

        def project(u, q):
            c, h = divmod(u, HALVES)
            if q == 0:
                gate_t[u] = gates_pool.tile([P, BLOCKS * ROWS], F32, name="gate_t", tag="gate_t")
                cand_t[u] = gates_pool.tile([P, BLOCKS * ROWS], F32, name="cand_t", tag="cand_t")
            m = BLOCKS * h + q
            pre = psum_pre.tile([P, ROWS], F32, name="pre", tag="pre")
            pairs = ((("w2", h), ("wx", c)), (("u2", h), ("uh", c)))
            for n, (weight, moving) in enumerate(pairs):
                nc.tensor.matmul_mx(
                    out=pre[:],
                    lhsT=codes[weight][:, q * P : (q + 1) * P].bitcast(FP8X4),
                    lhsT_scale=scales[weight][:, q * P : (q + 1) * P],
                    rhs=codes[moving][:].bitcast(FP8X4),
                    rhs_scale=scales[moving][:],
                    start=(n == 0),
                    stop=(n == 1),
                )
            cols = slice(q * ROWS, (q + 1) * ROWS)
            nc.scalar.activation(
                out=gate_t[u][:, cols], in_=pre[:], func=ACT.Sigmoid,
                bias=bias_t[:, m : m + 1], scale=1.0,
            )
            nc.scalar.activation(
                out=cand_t[u][:, cols], in_=pre[:], func=ACT.Tanh,
                bias=bias_t[:, 2 * BLOCKS + m : 2 * BLOCKS + m + 1], scale=1.0,
            )

        def candidate_term(u, a):
            cols = slice(2 * a * ROWS, (2 * a + 1) * ROWS)
            nc.vector.scalar_tensor_tensor(
                out=cand_t[u][:, cols], in0=gate_t[u][:, cols], scalar=kappa[:, 0:1],
                in1=cand_t[u][:, cols], op0=ALU.subtract, op1=ALU.mult,
            )
            cols = slice((2 * a + 1) * ROWS, (2 * a + 2) * ROWS)
            shifted = shift_pool.tile([P, ROWS], F32, name="shifted", tag="shifted")
            nc.gpsimd.tensor_scalar(
                out=shifted[:], in0=gate_t[u][:, cols], scalar1=one[:, 0:1],
                scalar2=neg_kappa[:, 0:1], op0=ALU.mult, op1=ALU.add,
            )
            nc.gpsimd.tensor_tensor(
                out=cand_t[u][:, cols], in0=shifted[:], in1=cand_t[u][:, cols], op=ALU.mult
            )

        def transpose_back(source, a):
            banks = []
            for j in range(2):
                i = 2 * a + j
                bank = psum_back.tile([P, ROWS], F32, name="bank", tag="bank")
                for q in range(BLOCKS):
                    nc.tensor.transpose(
                        bank[:, q * P : (q + 1) * P],
                        source[:, q * ROWS + i * P : q * ROWS + (i + 1) * P],
                        ident[:],
                    )
                banks.append(bank)
            return banks

        def span(u, a, j):
            start = (2 * a + j) * HIDDEN + (u % HALVES) * ROWS
            return slice(start, start + ROWS)

        def gate_times_state(u, a, banks):
            c, h = divmod(u, HALVES)
            if h == 0 and a == 0:
                out_sb[c] = out_pool.tile([P, BLOCKS * HIDDEN], F32, name="out_sb", tag="out_sb")
            for j in range(2):
                nc.vector.tensor_tensor(
                    out=out_sb[c][:, span(u, a, j)], in0=banks[j][:],
                    in1=state_sb[c][:, span(u, a, j)], op=ALU.mult,
                )

        def add_candidate(u, a, banks):
            c, h = divmod(u, HALVES)
            for j in range(2):
                nc.vector.scalar_tensor_tensor(
                    out=out_sb[c][:, span(u, a, j)], in0=banks[j][:], scalar=neg_sz[:, 0:1],
                    in1=out_sb[c][:, span(u, a, j)], op0=ALU.mult, op1=ALU.add,
                )
            if h == HALVES - 1:
                done = slice(2 * a * HIDDEN, 2 * (a + 1) * HIDDEN)
                nc.sync.dma_start(out=out_v[c][:, done], in_=out_sb[c][:, done])

        for k in range(4):
            load_operand(k)
        zeta_sb = const.tile([P, 1], BF16, name="zeta_sb")
        nu_sb = const.tile([P, 1], BF16, name="nu_sb")
        bias_rows = const.tile([P, P], BF16, name="bias_rows")
        nc.gpsimd.memset(bias_rows[:], 0.0)
        nc.scalar.dma_start(out=zeta_sb[:], in_=zeta.to_broadcast([P, 1]))
        nc.scalar.dma_start(out=nu_sb[:], in_=nu.to_broadcast([P, 1]))
        row_view = "o (m p) -> (o m) p"
        nc.scalar.dma_start(out=bias_rows[0 : 2 * BLOCKS, :], in_=bias_gate.rearrange(row_view, p=P))
        nc.scalar.dma_start(
            out=bias_rows[2 * BLOCKS : 4 * BLOCKS, :], in_=bias_update.rearrange(row_view, p=P)
        )
        for k in range(4, RAW_BUFS):
            load_operand(k)
        load_state(0)

        ident = const.tile([P, P], F32, name="ident")
        make_identity(nc, ident[:])

        sz = const.tile([P, 1], F32, name="sz")
        sn = const.tile([P, 1], F32, name="sn")
        inv_sz = const.tile([P, 1], F32, name="inv_sz")
        kappa = const.tile([P, 1], F32, name="kappa")
        neg_sz = const.tile([P, 1], F32, name="neg_sz")
        nc.scalar.activation(out=sz[:], in_=zeta_sb[:], func=ACT.Sigmoid)
        nc.scalar.activation(out=sn[:], in_=nu_sb[:], func=ACT.Sigmoid)
        nc.vector.tensor_scalar_max(out=sz[:], in0=sz[:], scalar1=TINY)
        nc.vector.reciprocal(out=inv_sz[:], in_=sz[:])
        nc.vector.tensor_add(out=kappa[:], in0=sz[:], in1=sn[:])
        nc.vector.tensor_mul(out=kappa[:], in0=kappa[:], in1=inv_sz[:])
        nc.vector.tensor_scalar_mul(out=neg_sz[:], in0=sz[:], scalar1=-1.0)
        neg_kappa = const.tile([P, 1], F32, name="neg_kappa")
        one = const.tile([P, 1], F32, name="one")
        nc.vector.tensor_scalar_mul(out=neg_kappa[:], in0=kappa[:], scalar1=-1.0)
        nc.vector.memset(one[:], 1.0)

        bias_rows_f = const.tile([P, P], F32, name="bias_rows_f")
        bias_t = const.tile([P, 4 * BLOCKS], F32, name="bias_t")
        nc.vector.tensor_copy(out=bias_rows_f[:], in_=bias_rows[:])
        bias_ps = psum_fwd.tile([P, 2 * 2 * P], F32, name="bias_ps", tag="flipped")
        nc.tensor.transpose(bias_ps[:, 0:P], bias_rows_f[:], ident[:])
        nc.vector.tensor_copy(out=bias_t[:], in_=bias_ps[:, 0 : 4 * BLOCKS])

        for s in range(FIRST_STEPS):
            transpose_step(s, on_vector=(s % 2 == 1))
            if s % 2 == 1:
                quantise(s // 2)
        steps_done = FIRST_STEPS

        for t in range(ROUNDS + LAG):
            u, a = divmod(t, 2)
            mixing = t >= LAG
            mixed_u, mixed_a = divmod(t - LAG, 2)
            if t % (2 * HALVES) == 0 and t // (2 * HALVES) + 1 < CHUNKS:
                load_state(t // (2 * HALVES) + 1)
            if t < ROUNDS:
                project(u, 2 * a)
            if mixing:
                gate_banks = transpose_back(gate_t[mixed_u], mixed_a)
            if t < ROUNDS:
                project(u, 2 * a + 1)
            if mixing:
                cand_banks = transpose_back(cand_t[mixed_u], mixed_a)
            steps_due = min(total_steps, steps_done + 2, t + 1 + LEAD)
            finished = []
            while steps_done < steps_due:
                transpose_step(steps_done, on_vector=(not mixing))
                if steps_done % 2 == 1:
                    finished.append(steps_done // 2)
                steps_done += 1
            if mixing:
                gate_times_state(mixed_u, mixed_a, gate_banks)
            if 1 <= t <= ROUNDS:
                candidate_term((t - 1) // 2, (t - 1) % 2)
            if mixing:
                add_candidate(mixed_u, mixed_a, cand_banks)
            for k in finished:
                quantise(k)
